import numpy as np
import ml_dtypes


def mxq(x, axis, fmt="e4m3"):
    dtype, down = {"e4m3": (ml_dtypes.float8_e4m3fn, 7), "e5m2": (ml_dtypes.float8_e5m2, 14)}[fmt]
    v = np.moveaxis(np.asarray(x, np.float32).astype(ml_dtypes.bfloat16).astype(np.float64), axis, -1)
    blocks = v.reshape(v.shape[:-1] + (-1, 32))
    amax = np.abs(blocks).max(-1, keepdims=True)
    byte = np.maximum(np.where(amax > 0, np.frexp(amax)[1] - 1 + 127, 0) - down, 1)
    scale = np.exp2(byte - 127.0)
    codes = (blocks / scale).astype(np.float32).astype(dtype).astype(np.float64)
    return np.moveaxis((codes * scale).reshape(v.shape), -1, axis)


WIDE = False


def mx_kscale(k, group=512):
    if not WIDE:
        return np.ones(k)
    levels = np.array([18, -18])
    if group != 512:
        return np.exp2(np.random.permutation(np.resize(levels, k // group))).repeat(group)
    if k % 512:
        return np.exp2(np.random.permutation(np.resize(levels, k // 32))).repeat(32)
    a = np.empty((k // 512, 16))
    for p in range(k // 512):
        a[p, :8] = np.random.permutation(np.resize(levels, 8))
        for g in range(8):
            far = levels[np.abs(levels - a[p, g]) >= 10]
            a[p, g + 8] = far[np.random.randint(len(far))]
    return np.exp2(a.ravel()).repeat(32)


BF16 = ml_dtypes.bfloat16


def bf(x):
    return np.asarray(x, np.float32).astype(BF16)


def f64(x):
    return np.asarray(x).astype(np.float64)


B, F, C, H = 2, 1024, 512, 512
K = C + H
T = B * F


def sigmoid(v):
    return 1.0 / (1.0 + np.exp(-v))


def gate_values(x, hidden_state, W_f, b_f, W_i, b_i, W_o, b_o, W_g, b_g):
    xh = np.concatenate([np.swapaxes(f64(x), 1, 2), f64(hidden_state)], axis=1)
    W = np.concatenate([f64(W_f), f64(W_i), f64(W_g), f64(W_o)], axis=0)
    b = np.concatenate([f64(b_f), f64(b_i), f64(b_g), f64(b_o)], axis=0)
    return W @ xh + b[None, :, None]


def setup_inputs():
    s = mx_kscale(T).reshape(B, F)
    u = mx_kscale(H, group=128)

    def w():
        return bf(np.random.standard_normal((H, K)) / np.sqrt(K))

    def b():
        return bf(np.random.standard_normal(H) * 0.3)

    x0 = bf(np.random.standard_normal((B, F, C)))
    h0 = bf(np.random.standard_normal((B, H, F)))
    cell_state = bf(np.random.standard_normal((B, H, F)))
    wf0, b_f = w(), b()
    wi0, b_i = w(), b()
    wo0, b_o = w(), b()
    wg0, b_g = w(), b()
    g = np.random.standard_normal((B, F, H)) * np.exp2(np.random.randint(-6, 1, (B, F, 1))) * 8.0
    gates = gate_values(x0, h0, wf0, b_f, wi0, b_i, wo0, b_o, wg0, b_g)
    return {"x": bf(f64(x0) * s[:, :, None]),
            "hidden_state": bf(f64(h0) * s[:, None, :]),
            "cell_state": cell_state,
            "W_f": bf(f64(wf0) / u[:, None]), "b_f": b_f,
            "W_i": bf(f64(wi0) / u[:, None]), "b_i": b_i,
            "W_o": bf(f64(wo0) / u[:, None]), "b_o": b_o,
            "W_g": bf(f64(wg0) / u[:, None]), "b_g": b_g,
            "gates": np.asarray(gates, np.float32),
            "grad_out": bf(g / s[:, :, None] * u[None, None, :])}


def reference(x, hidden_state, cell_state, W_f, b_f, W_i, b_i, W_o, b_o, W_g, b_g, gates, grad_out):
    z = f64(gates)
    f_t = sigmoid(z[:, 0 * H:1 * H])
    i_t = sigmoid(z[:, 1 * H:2 * H])
    g_t = np.tanh(z[:, 2 * H:3 * H])
    o_t = sigmoid(z[:, 3 * H:4 * H])
    cell = f64(cell_state)
    th = np.tanh(cell * f_t + i_t * g_t)
    gh = np.swapaxes(f64(grad_out), 1, 2)
    dc = gh * o_t * (1.0 - th * th)
    dz_f = dc * cell * f_t * (1.0 - f_t)
    dz_i = dc * g_t * i_t * (1.0 - i_t)
    dz_g = dc * i_t * (1.0 - g_t * g_t)
    dz_o = gh * th * o_t * (1.0 - o_t)
    dz = np.swapaxes(np.concatenate([dz_f, dz_i, dz_g, dz_o], axis=1), 1, 2).reshape(T, 4 * H)
    Wx = np.concatenate([f64(W_f)[:, :C], f64(W_i)[:, :C], f64(W_g)[:, :C], f64(W_o)[:, :C]], axis=0)
    dx = (mxq(dz, 1, "e5m2") @ mxq(Wx, 0, "e4m3")).reshape(B, F, C)
    xh = np.concatenate([f64(x).reshape(T, C), np.swapaxes(f64(hidden_state), 1, 2).reshape(T, H)], axis=1)
    dW_f = mxq(dz[:, :H], 0, "e5m2").T @ mxq(xh, 0, "e4m3")
    return dx, dW_f

@@ -1,0 +1,419 @@
+from contextlib import ExitStack
+
+import concourse.mybir as mybir
+from concourse.masks import make_identity
+
+F32 = mybir.dt.float32
+BF16 = mybir.dt.bfloat16
+U32 = mybir.dt.uint32
+U8 = mybir.dt.uint8
+E4 = mybir.dt.float8_e4m3fn_x4
+E5 = mybir.dt.float8_e5m2_x4
+ALU = mybir.AluOpType
+ACT = mybir.ActivationFunctionType
+ENG = mybir.EngineType
+
+B, F, C, H = 2, 1024, 512, 512
+T = B * F
+P = 128
+J = 4
+PASS = P * J
+
+FLOPS = 2 * T * (4 * H) * C + 2 * H * T * (C + H)
+BYTES = 4 * B * 4 * H * F + 2 * (4 * B * F * H + 4 * H * C) + 4 * (T * C + H * (C + H))
+
+N = 256
+TILES = T // N
+PER_PASS = PASS // N
+
+
+def tile_batchedlstm_v_kernel(
+    tc, x, hidden_state, cell_state, W_f, b_f, W_i, b_i, W_o, b_o, W_g, b_g, gates, grad_out, out_0, out_1
+):
+    nc = tc.nc
+    weights = [W_f, W_i, W_g, W_o]
+
+    with ExitStack() as ctx:
+        keep = ctx.enter_context(tc.tile_pool(name="keep", bufs=1))
+        work = ctx.enter_context(tc.tile_pool(name="work", bufs=2))
+        psum = ctx.enter_context(tc.psum_pool(name="psum", bufs=1))
+
+        ident = keep.tile([P, P], F32, tag="ident")
+        wq = keep.tile([P, 4, C], U32, tag="wq", align_bytes=64)
+        ws = keep.tile([P, 4, C], U8, tag="ws", align_bytes=64)
+        xq = keep.tile([P, 4, 2, 512], U32, tag="xq", align_bytes=64)
+        xs = keep.tile([P, 4, 2, 512], U8, tag="xs", align_bytes=64)
+        fq = keep.tile([P, 4, H], U32, tag="fq", align_bytes=64)
+        fs = keep.tile([P, 4, H], U8, tag="fs", align_bytes=64)
+        warm = keep.tile([P, 8], F32, tag="warm")
+
+        make_identity(nc, ident[:])
+        nc.vector.memset(warm[:], 0.0)
+        nc.scalar.activation(out=warm[:], in_=warm[:], func=ACT.Sigmoid)
+
+        st = [dict() for t in range(TILES + 1)]
+        half = [dict() for g in range(4)]
+
+        def place(t):
+            b, f0 = divmod(t * N, F)
+            return b, f0
+
+        def load_half(g):
+            b, f0 = divmod(g * PASS, F)
+            cell = work.tile([P, J, PASS], BF16, tag="cell", bufs=2)
+            nc.sync.dma_start(
+                out=cell[:], in_=cell_state[b].rearrange("(p j) f -> p j f", j=J)[:, :, f0 : f0 + PASS]
+            )
+            go = work.tile([P, 4, H], BF16, tag="gout", bufs=2)
+            nc.sync.dma_start(out=go[:], in_=grad_out[b, f0 : f0 + PASS, :].rearrange("(m p) h -> p m h", p=P))
+            half[g]["cell"] = cell
+            half[g]["gout"] = go
+
+        def load_gate(t, gi):
+            b, f0 = place(t)
+            z = work.tile([P, J, N], F32, tag="z" + str(gi), bufs=2)
+            src = gates[b, gi * H : (gi + 1) * H, f0 : f0 + N].rearrange("(p j) f -> p j f", j=J)
+            nc.sync.dma_start(out=z[:], in_=src)
+            st[t]["z" + str(gi)] = z
+
+        def load_w(gi):
+            raw = work.tile([P, J, C], BF16, tag="raw", bufs=2)
+            nc.sync.dma_start(out=raw[:], in_=weights[gi][:, 0:C].rearrange("(p j) c -> p j c", j=J))
+            half[gi]["w"] = raw
+
+        def load_x(g):
+            b, f0 = divmod(g * PASS, F)
+            raw = work.tile([P, J, C], BF16, tag="raw", bufs=2)
+            nc.sync.dma_start(out=raw[:], in_=x[b, f0 : f0 + PASS, :].rearrange("(p j) c -> p j c", j=J))
+            half[g]["x"] = raw
+
+        def load_hidden(b):
+            raw = work.tile([P, 4, F], BF16, tag="hraw", bufs=1)
+            nc.sync.dma_start(out=raw[:], in_=hidden_state[b].rearrange("(m p) f -> p m f", p=P))
+            half[2 * b]["h"] = raw
+            half[2 * b + 1]["h"] = raw
+
+        def interleave(eng, raw):
+            grp = work.tile([P, C, J], BF16, tag="grp", bufs=2, align_bytes=64)
+            dst = grp[:].rearrange("p (c i) j -> p c j i", i=4)
+            src = raw[:].rearrange("p j (c i) -> p c j i", i=4)
+            if eng == "v":
+                nc.vector.tensor_copy(out=dst, in_=src)
+            else:
+                nc.scalar.copy(out=dst, in_=src)
+            return grp
+
+        def flat(t3):
+            return t3[:].rearrange("p c j -> p (c j)")
+
+        def quant_w(gi):
+            nc.vector.quantize_mx(out=wq[:, gi, :].bitcast(E4), scales=ws[:, gi, :], in_=flat(half[gi]["wg"]))
+
+        def quant_x(g):
+            nc.vector.quantize_mx(out=xq[:, g, 0, :].bitcast(E4), scales=xs[:, g, 0, :], in_=flat(half[g]["xg"]))
+
+        def acts(t):
+            s = st[t]
+            for gi, nm, fn in ((0, "f", ACT.Sigmoid), (1, "i", ACT.Sigmoid), (2, "g", ACT.Tanh), (3, "o", ACT.Sigmoid)):
+                v = work.tile([P, N, J], F32, tag=nm, bufs=2)
+                nc.scalar.activation(
+                    out=v[:].rearrange("p (c i) j -> p c j i", i=4),
+                    in_=s["z" + str(gi)][:].rearrange("p j (c i) -> p c j i", i=4),
+                    func=fn,
+                )
+                s[nm] = v
+            g2 = work.tile([P, N, J], F32, tag="g2", bufs=1)
+            nc.scalar.activation(out=flat(g2), in_=flat(s["g"]), func=ACT.Square)
+            s["g2"] = g2
+
+        def va(t):
+            s = st[t]
+            l0 = (t % PER_PASS) * N
+            a = work.tile([P, N, J], F32, tag="a", bufs=1)
+            cell = half[t // PER_PASS]["cell"]
+            nc.vector.tensor_tensor(
+                out=a[:], in0=cell[:, :, l0 : l0 + N].rearrange("p j f -> p f j"), in1=s["f"][:], op=ALU.mult
+            )
+            bb = work.tile([P, N, J], F32, tag="b", bufs=1)
+            nc.vector.tensor_tensor(out=bb[:], in0=s["i"][:], in1=s["g"][:], op=ALU.mult)
+            s["a"] = a
+            s["b"] = bb
+
+        def minus_one_times(out, in0, in1):
+            nc.vector.scalar_tensor_tensor(out=out, in0=in0, scalar=1.0, in1=in1, op0=ALU.subtract, op1=ALU.mult)
+
+        def cT(t):
+            s = st[t]
+            th = work.tile([P, N * J], F32, tag="thT", bufs=1)
+            sq = work.tile([P, N * J], F32, tag="sqT", bufs=1)
+            for h in range(N * J // 512):
+                ps = psum.tile([P, 512], F32, tag="cT", bufs=1)
+                for k in range(4):
+                    cols = slice(h * 512 + k * P, h * 512 + (k + 1) * P)
+                    dst = ps[:, k * P : (k + 1) * P]
+                    nc.tensor.matmul(
+                        out=dst, lhsT=flat(s["a"])[:, cols], rhs=ident[:], is_transpose=True, start=True, stop=False
+                    )
+                    nc.tensor.matmul(
+                        out=dst, lhsT=flat(s["b"])[:, cols], rhs=ident[:], is_transpose=True, start=False, stop=True
+                    )
+                hs = slice(h * 512, (h + 1) * 512)
+                nc.scalar.activation(out=th[:, hs], in_=ps[:], func=ACT.Tanh, scale=-1.0)
+            nc.scalar.activation(out=sq[:], in_=th[:], func=ACT.Square)
+            s["thT"] = th
+            s["sqT"] = sq
+
+        def back(t):
+            s = st[t]
+            for nm in ("sq", "th"):
+                s[nm] = []
+                for h in range(N * J // 512):
+                    ps = psum.tile([P, 512], F32, tag="bk", bufs=4)
+                    for k in range(4):
+                        c0 = h * 512 + k * P
+                        nc.tensor.transpose(ps[:, k * P : (k + 1) * P], s[nm + "T"][:, c0 : c0 + P], ident[:])
+                    s[nm].append(ps)
+
+        def gh(t):
+            s = st[t]
+            ps = psum.tile([P, 2, N], F32, tag="mm", bufs=3)
+            words = half[t // PER_PASS]["gout"][:].rearrange("p m h -> p (m h)").bitcast(F32)
+            m0 = (t % PER_PASS) * (N // P)
+            for m in range(N // P):
+                for u in range(2):
+                    w0 = (m0 + m) * (H // 2) + u
+                    nc.tensor.transpose(
+                        ps[:, u, m * P : (m + 1) * P], words[:, w0 : (m0 + m + 1) * (H // 2) : 2], ident[:]
+                    )
+            s["gh"] = ps
+
+        def vgo(t):
+            s = st[t]
+            go = work.tile([P, N, J], F32, tag="go", bufs=2)
+            nc.vector.tensor_tensor(
+                out=go[:].rearrange("p f (u e) -> p f u e", e=2),
+                in0=s["gh"][:].rearrange("p u f -> p (u f)").bitcast(BF16).rearrange("p (u f e) -> p f u e", u=2, e=2),
+                in1=s["o"][:].rearrange("p f (u e) -> p f u e", e=2),
+                op=ALU.mult,
+            )
+            s["go"] = go
+
+        def b_ndc(t):
+            s = st[t]
+            ndc = work.tile([P, N, J], F32, tag="ndc", bufs=1)
+            for h in range(N * J // 512):
+                hs = slice(h * 512, (h + 1) * 512)
+                minus_one_times(flat(ndc)[:, hs], s["sq"][h][:], flat(s["go"])[:, hs])
+            s["ndc"] = ndc
+            if t % PER_PASS == 0:
+                dzf = work.tile([P, PASS, J], BF16, tag="dzf", bufs=2, align_bytes=64)
+                half[t // PER_PASS]["dzf"] = dzf
+            dz = work.tile([P, 3, N * J], BF16, tag="dz", bufs=2, align_bytes=64)
+            s["dz"] = dz
+
+        def dzf_slice(t):
+            l0 = (t % PER_PASS) * N
+            return flat(half[t // PER_PASS]["dzf"])[:, l0 * J : (l0 + N) * J]
+
+        def b_o(t):
+            s = st[t]
+            for h in range(N * J // 512):
+                hs = slice(h * 512, (h + 1) * 512)
+                nc.vector.tensor_tensor(
+                    out=s["dz"][:, 2, hs], in0=s["th"][h][:], in1=flat(s["o"])[:, hs], op=ALU.mult
+                )
+
+        def quants(t):
+            s = st[t]
+            dq = work.tile([P, 4, N], U32, tag="dq", bufs=2, align_bytes=64)
+            ds = work.tile([P, 4, N], U8, tag="ds", bufs=2, align_bytes=64)
+            nc.vector.quantize_mx(
+                out=dq[:, 1:3, :].rearrange("p g n -> p (g n)").bitcast(E5),
+                scales=ds[:, 1:3, :].rearrange("p g n -> p (g n)"),
+                in_=s["dz"][:, 0:2, :].rearrange("p g n -> p (g n)"),
+            )
+            nc.vector.quantize_mx(out=dq[:, 3, :].bitcast(E5), scales=ds[:, 3, :], in_=s["dz"][:, 2, :])
+            nc.vector.quantize_mx(out=dq[:, 0, :].bitcast(E5), scales=ds[:, 0, :], in_=dzf_slice(t))
+            s["dq"] = dq
+            s["ds"] = ds
+
+        def out0_mm(t):
+            s = st[t]
+            s["acc"] = []
+            for m in range(N // P):
+                ps = psum.tile([P, C], F32, tag="mm", bufs=3)
+                ms = slice(m * P, (m + 1) * P)
+                for k, gi in enumerate((1, 2, 3, 0)):
+                    nc.tensor.matmul_mx(
+                        out=ps[:],
+                        lhsT=s["dq"][:, gi, ms].bitcast(E5),
+                        lhsT_scale=s["ds"][:, gi, ms],
+                        rhs=wq[:, gi, :].bitcast(E4),
+                        rhs_scale=ws[:, gi, :],
+                        start=(k == 0),
+                        stop=(k == 3),
+                    )
+                s["acc"].append(ps)
+
+        def out0_evac(t, engs):
+            s = st[t]
+            b, f0 = place(t)
+            for m in range(N // P):
+                o = work.tile([P, C], F32, tag="osb", bufs=4)
+                if engs[m % len(engs)] == "s":
+                    nc.scalar.copy(out=o[:], in_=s["acc"][m][:])
+                else:
+                    nc.vector.tensor_copy(out=o[:], in_=s["acc"][m][:])
+                nc.sync.dma_start(out=out_0[b, f0 + m * P : f0 + (m + 1) * P, :], in_=o[:])
+
+        def hid(g):
+            words = half[g]["h"][:].rearrange("p m f -> p (m f)").bitcast(F32)
+            grp = work.tile([P, H, J], BF16, tag="hgrp", bufs=1, align_bytes=64)
+            gw = flat(grp).bitcast(F32).rearrange("p (r u) -> p r u", u=2)
+            s0 = (g % 2) * (PASS // 2)
+            for mm in range(2):
+                ps = psum.tile([P, 2, 2 * P], F32, tag="mm", bufs=3)
+                for m in range(2):
+                    for u in range(2):
+                        w0 = (2 * mm + m) * (F // 2) + s0
+                        nc.tensor.transpose(
+                            ps[:, u, m * P : (m + 1) * P], words[:, w0 + u : w0 + PASS // 2 : 2], ident[:]
+                        )
+                nc.scalar.copy(out=gw[:, mm * 2 * P : (mm + 1) * 2 * P, :], in_=ps[:].rearrange("p u r -> p r u"))
+            half[g]["hg"] = grp
+
+        def quant_h(g):
+            nc.vector.quantize_mx(out=xq[:, g, 1, :].bitcast(E4), scales=xs[:, g, 1, :], in_=flat(half[g]["hg"]))
+
+        def dft(g, engs):
+            words = flat(half[g]["dzf"]).bitcast(F32).rearrange("p (q t w) -> p t w q", t=J, w=2)
+            grp = work.tile([P, 2, 2, P, J], BF16, tag="dft", bufs=1, align_bytes=64)
+            for w in range(2):
+                ps = psum.tile([P, J, P], F32, tag="mm", bufs=3)
+                for t in range(J):
+                    nc.tensor.transpose(ps[:, t, :], words[:, t, w, :], ident[:])
+                src = ps[:].rearrange("p t m -> p (t m)").bitcast(BF16).rearrange("p (t m e) -> p e m t", t=J, e=2)
+                if engs[w] == "s":
+                    nc.scalar.copy(out=grp[:, w], in_=src)
+                else:
+                    nc.vector.tensor_copy(out=grp[:, w], in_=src)
+            half[g]["fg"] = grp
+
+        def quant_ft(g):
+            nc.vector.quantize_mx(
+                out=fq[:, g, :].bitcast(E5),
+                scales=fs[:, g, :],
+                in_=half[g]["fg"][:].rearrange("p w e m t -> p (w e m t)"),
+            )
+
+        out1_view = out_1.rearrange("(m j) k -> j m k", j=J)
+
+        def out1(j, kh, tag, bufs, eng):
+            ps = psum.tile([P, 512], F32, tag=tag, bufs=bufs)
+            js = slice(j * P, (j + 1) * P)
+            for g in range(4):
+                nc.tensor.matmul_mx(
+                    out=ps[:],
+                    lhsT=fq[:, g, js].bitcast(E5),
+                    lhsT_scale=fs[:, g, js],
+                    rhs=xq[:, g, kh, :].bitcast(E4),
+                    rhs_scale=xs[:, g, kh, :],
+                    start=(g == 0),
+                    stop=(g == 3),
+                )
+            o = work.tile([P, C], F32, tag="osb", bufs=4)
+            if eng == "s":
+                nc.scalar.copy(out=o[:], in_=ps[:])
+            else:
+                nc.vector.tensor_copy(out=o[:], in_=ps[:])
+            nc.sync.dma_start(out=out1_view[j][:, kh * 512 : (kh + 1) * 512], in_=o[:])
+
+        for unused in range(1):
+            load_gate(0, 0)
+            load_half(0)
+            load_gate(0, 1)
+            load_gate(0, 2)
+            load_gate(0, 3)
+            load_w(0)
+            load_w(1)
+            for gi in range(4):
+                load_gate(1, gi)
+            load_w(2)
+            load_w(3)
+            acts(0)
+            gh(0)
+            half[0]["wg"] = interleave("v", half[0]["w"])
+
+            for t in range(TILES + 1):
+                last = t == TILES
+                if t + 2 < TILES:
+                    for gi in range(4):
+                        load_gate(t + 2, gi)
+                    if (t + 2) % PER_PASS == 0:
+                        load_half((t + 2) // PER_PASS)
+                if 1 <= t <= 4:
+                    load_x(t - 1)
+                if t in (1, 4):
+                    load_hidden((t - 1) // 3)
+
+                if not last:
+                    va(t)
+                    cT(t)
+                if t == 0:
+                    half[1]["wg"] = interleave("v", half[1]["w"])
+                    quant_w(0)
+                if t > 0:
+                    b_ndc(t - 1)
+                    p = st[t - 1]
+                    if last:
+                        nc.vector.tensor_tensor(out=dzf_slice(t - 1), in0=flat(p["f"]), in1=flat(p["ndc"]), op=ALU.mult)
+                    else:
+                        nc.gpsimd.tensor_tensor(out=dzf_slice(t - 1), in0=flat(p["f"]), in1=flat(p["ndc"]), op=ALU.mult)
+                    b_o(t - 1)
+                if not last:
+                    vgo(t)
+                if t > 0:
+                    nc.vector.tensor_tensor(out=p["dz"][:, 0, :], in0=flat(p["g"]), in1=flat(p["ndc"]), op=ALU.mult)
+                    nc.vector.tensor_tensor(out=p["dz"][:, 1, :], in0=flat(p["i"]), in1=flat(p["ndc"]), op=ALU.mult)
+                if not last:
+                    s = st[t]
+                    minus_one_times(flat(s["f"]), flat(s["f"]), flat(s["a"]))
+                if t == 0:
+                    quant_w(1)
+                if t == 1:
+                    quant_w(2)
+                    quant_w(3)
+                if last:
+                    dft(3, "sv")
+                    quant_ft(3)
+                if t > 0:
+                    quants(t - 1)
+                if not last:
+                    minus_one_times(flat(s["g"]), flat(s["i"]), flat(s["b"]))
+                    minus_one_times(flat(s["i"]), flat(s["g2"]), flat(s["i"]))
+                    minus_one_times(flat(s["o"]), flat(s["o"]), flat(s["go"]))
+                if t + 1 < TILES:
+                    acts(t + 1)
+                    gh(t + 1)
+                if t == 0:
+                    half[2]["wg"] = interleave("s", half[2]["w"])
+                    half[3]["wg"] = interleave("s", half[3]["w"])
+                if not last and t > 0:
+                    if t % PER_PASS == 0:
+                        dft(t // PER_PASS - 1, "ss")
+                        quant_ft(t // PER_PASS - 1)
+                    if 2 <= t <= 5:
+                        half[t - 2]["xg"] = interleave("s", half[t - 2]["x"])
+                        quant_x(t - 2)
+                    if t in (2, 3, 5, 6):
+                        g = {2: 0, 3: 1, 5: 2, 6: 3}[t]
+                        hid(g)
+                        quant_h(g)
+                    out0_mm(t - 1)
+                    out0_evac(t - 1, "s")
+                if not last:
+                    back(t)
+            out0_mm(TILES - 1)
+            out0_evac(TILES - 1, "vs")
+            for k in range(8):
+                out1(k % 4, k // 4, "bk", 4, "sv"[k % 2])

@@ -22,9 +22,12 @@ PASS = P * J
 FLOPS = 2 * T * (4 * H) * C + 2 * H * T * (C + H)
 BYTES = 4 * B * 4 * H * F + 2 * (4 * B * F * H + 4 * H * C) + 4 * (T * C + H * (C + H))
 
-N = 256
-TILES = T // N
-PER_PASS = PASS // N
+SIZES = [128, 128, 256, 256, 256, 256, 256, 256, 128, 128]
+STARTS = [sum(SIZES[:k]) for k in range(len(SIZES))]
+TILES = len(SIZES)
+X_AT = [2, 3, 4, 5]
+H_AT = [2, 3, 5, 6]
+PART_AT = [7, 7, 7, 8, 8, 8, 9, 9]
 
 
 def tile_batchedlstm_v_kernel(
@@ -51,39 +54,45 @@ def tile_batchedlstm_v_kernel(
         nc.vector.memset(warm[:], 0.0)
         nc.scalar.activation(out=warm[:], in_=warm[:], func=ACT.Sigmoid)
 
-        st = [dict() for t in range(TILES + 1)]
+        st = [dict(n=SIZES[t], tok=STARTS[t], pa=STARTS[t] // PASS, l=STARTS[t] % PASS) for t in range(TILES)]
         half = [dict() for g in range(4)]
 
-        def place(t):
-            b, f0 = divmod(t * N, F)
-            return b, f0
+        def flat(t3):
+            return t3[:].rearrange("p c j -> p (c j)")
 
-        def load_half(g):
+        def load_half(g, parts):
             b, f0 = divmod(g * PASS, F)
-            cell = work.tile([P, J, PASS], BF16, tag="cell", bufs=2)
+            if "cell" not in half[g]:
+                cell = work.tile([P, J, PASS], BF16, tag="cell", bufs=2)
+                go = work.tile([P, 4, H], BF16, tag="gout", bufs=2)
+                half[g]["cell"] = cell
+                half[g]["gout"] = go
+            m0, m1 = parts
             nc.sync.dma_start(
-                out=cell[:], in_=cell_state[b].rearrange("(p j) f -> p j f", j=J)[:, :, f0 : f0 + PASS]
+                out=half[g]["cell"][:, :, m0 * P : m1 * P],
+                in_=cell_state[b].rearrange("(p j) f -> p j f", j=J)[:, :, f0 + m0 * P : f0 + m1 * P],
             )
-            go = work.tile([P, 4, H], BF16, tag="gout", bufs=2)
-            nc.sync.dma_start(out=go[:], in_=grad_out[b, f0 : f0 + PASS, :].rearrange("(m p) h -> p m h", p=P))
-            half[g]["cell"] = cell
-            half[g]["gout"] = go
+            nc.sync.dma_start(
+                out=half[g]["gout"][:, m0:m1, :],
+                in_=grad_out[b, f0 + m0 * P : f0 + m1 * P, :].rearrange("(m p) h -> p m h", p=P),
+            )
 
         def load_gate(t, gi):
-            b, f0 = place(t)
-            z = work.tile([P, J, N], F32, tag="z" + str(gi), bufs=2)
-            src = gates[b, gi * H : (gi + 1) * H, f0 : f0 + N].rearrange("(p j) f -> p j f", j=J)
+            n = st[t]["n"]
+            b, f0 = divmod(st[t]["tok"], F)
+            z = work.tile([P, J, n], F32, tag="z" + str(gi), bufs=2)
+            src = gates[b, gi * H : (gi + 1) * H, f0 : f0 + n].rearrange("(p j) f -> p j f", j=J)
             nc.sync.dma_start(out=z[:], in_=src)
             st[t]["z" + str(gi)] = z
 
         def load_w(gi):
-            raw = work.tile([P, J, C], BF16, tag="raw", bufs=2)
+            raw = work.tile([P, J, C], BF16, tag="raw", bufs=2, align_bytes=64)
             nc.sync.dma_start(out=raw[:], in_=weights[gi][:, 0:C].rearrange("(p j) c -> p j c", j=J))
             half[gi]["w"] = raw
 
         def load_x(g):
             b, f0 = divmod(g * PASS, F)
-            raw = work.tile([P, J, C], BF16, tag="raw", bufs=2)
+            raw = work.tile([P, J, C], BF16, tag="raw", bufs=2, align_bytes=64)
             nc.sync.dma_start(out=raw[:], in_=x[b, f0 : f0 + PASS, :].rearrange("(p j) c -> p j c", j=J))
             half[g]["x"] = raw
 
@@ -103,174 +112,22 @@ def tile_batchedlstm_v_kernel(
                 nc.scalar.copy(out=dst, in_=src)
             return grp
 
-        def flat(t3):
-            return t3[:].rearrange("p c j -> p (c j)")
+        def ilv_w(gi, eng):
+            half[gi]["wg"] = interleave(eng, half[gi]["w"])
 
         def quant_w(gi):
             nc.vector.quantize_mx(out=wq[:, gi, :].bitcast(E4), scales=ws[:, gi, :], in_=flat(half[gi]["wg"]))
 
+        def ilv_x(g, eng):
+            half[g]["xg"] = interleave(eng, half[g]["x"])
+
         def quant_x(g):
             nc.vector.quantize_mx(out=xq[:, g, 0, :].bitcast(E4), scales=xs[:, g, 0, :], in_=flat(half[g]["xg"]))
 
-        def acts(t):
-            s = st[t]
-            for gi, nm, fn in ((0, "f", ACT.Sigmoid), (1, "i", ACT.Sigmoid), (2, "g", ACT.Tanh), (3, "o", ACT.Sigmoid)):
-                v = work.tile([P, N, J], F32, tag=nm, bufs=2)
-                nc.scalar.activation(
-                    out=v[:].rearrange("p (c i) j -> p c j i", i=4),
-                    in_=s["z" + str(gi)][:].rearrange("p j (c i) -> p c j i", i=4),
-                    func=fn,
-                )
-                s[nm] = v
-            g2 = work.tile([P, N, J], F32, tag="g2", bufs=1)
-            nc.scalar.activation(out=flat(g2), in_=flat(s["g"]), func=ACT.Square)
-            s["g2"] = g2
-
-        def va(t):
-            s = st[t]
-            l0 = (t % PER_PASS) * N
-            a = work.tile([P, N, J], F32, tag="a", bufs=1)
-            cell = half[t // PER_PASS]["cell"]
-            nc.vector.tensor_tensor(
-                out=a[:], in0=cell[:, :, l0 : l0 + N].rearrange("p j f -> p f j"), in1=s["f"][:], op=ALU.mult
-            )
-            bb = work.tile([P, N, J], F32, tag="b", bufs=1)
-            nc.vector.tensor_tensor(out=bb[:], in0=s["i"][:], in1=s["g"][:], op=ALU.mult)
-            s["a"] = a
-            s["b"] = bb
-
-        def minus_one_times(out, in0, in1):
-            nc.vector.scalar_tensor_tensor(out=out, in0=in0, scalar=1.0, in1=in1, op0=ALU.subtract, op1=ALU.mult)
-
-        def cT(t):
-            s = st[t]
-            th = work.tile([P, N * J], F32, tag="thT", bufs=1)
-            sq = work.tile([P, N * J], F32, tag="sqT", bufs=1)
-            for h in range(N * J // 512):
-                ps = psum.tile([P, 512], F32, tag="cT", bufs=1)
-                for k in range(4):
-                    cols = slice(h * 512 + k * P, h * 512 + (k + 1) * P)
-                    dst = ps[:, k * P : (k + 1) * P]
-                    nc.tensor.matmul(
-                        out=dst, lhsT=flat(s["a"])[:, cols], rhs=ident[:], is_transpose=True, start=True, stop=False
-                    )
-                    nc.tensor.matmul(
-                        out=dst, lhsT=flat(s["b"])[:, cols], rhs=ident[:], is_transpose=True, start=False, stop=True
-                    )
-                hs = slice(h * 512, (h + 1) * 512)
-                nc.scalar.activation(out=th[:, hs], in_=ps[:], func=ACT.Tanh, scale=-1.0)
-            nc.scalar.activation(out=sq[:], in_=th[:], func=ACT.Square)
-            s["thT"] = th
-            s["sqT"] = sq
-
-        def back(t):
-            s = st[t]
-            for nm in ("sq", "th"):
-                s[nm] = []
-                for h in range(N * J // 512):
-                    ps = psum.tile([P, 512], F32, tag="bk", bufs=4)
-                    for k in range(4):
-                        c0 = h * 512 + k * P
-                        nc.tensor.transpose(ps[:, k * P : (k + 1) * P], s[nm + "T"][:, c0 : c0 + P], ident[:])
-                    s[nm].append(ps)
-
-        def gh(t):
-            s = st[t]
-            ps = psum.tile([P, 2, N], F32, tag="mm", bufs=3)
-            words = half[t // PER_PASS]["gout"][:].rearrange("p m h -> p (m h)").bitcast(F32)
-            m0 = (t % PER_PASS) * (N // P)
-            for m in range(N // P):
-                for u in range(2):
-                    w0 = (m0 + m) * (H // 2) + u
-                    nc.tensor.transpose(
-                        ps[:, u, m * P : (m + 1) * P], words[:, w0 : (m0 + m + 1) * (H // 2) : 2], ident[:]
-                    )
-            s["gh"] = ps
-
-        def vgo(t):
-            s = st[t]
-            go = work.tile([P, N, J], F32, tag="go", bufs=2)
-            nc.vector.tensor_tensor(
-                out=go[:].rearrange("p f (u e) -> p f u e", e=2),
-                in0=s["gh"][:].rearrange("p u f -> p (u f)").bitcast(BF16).rearrange("p (u f e) -> p f u e", u=2, e=2),
-                in1=s["o"][:].rearrange("p f (u e) -> p f u e", e=2),
-                op=ALU.mult,
-            )
-            s["go"] = go
-
-        def b_ndc(t):
-            s = st[t]
-            ndc = work.tile([P, N, J], F32, tag="ndc", bufs=1)
-            for h in range(N * J // 512):
-                hs = slice(h * 512, (h + 1) * 512)
-                minus_one_times(flat(ndc)[:, hs], s["sq"][h][:], flat(s["go"])[:, hs])
-            s["ndc"] = ndc
-            if t % PER_PASS == 0:
-                dzf = work.tile([P, PASS, J], BF16, tag="dzf", bufs=2, align_bytes=64)
-                half[t // PER_PASS]["dzf"] = dzf
-            dz = work.tile([P, 3, N * J], BF16, tag="dz", bufs=2, align_bytes=64)
-            s["dz"] = dz
-
-        def dzf_slice(t):
-            l0 = (t % PER_PASS) * N
-            return flat(half[t // PER_PASS]["dzf"])[:, l0 * J : (l0 + N) * J]
-
-        def b_o(t):
-            s = st[t]
-            for h in range(N * J // 512):
-                hs = slice(h * 512, (h + 1) * 512)
-                nc.vector.tensor_tensor(
-                    out=s["dz"][:, 2, hs], in0=s["th"][h][:], in1=flat(s["o"])[:, hs], op=ALU.mult
-                )
-
-        def quants(t):
-            s = st[t]
-            dq = work.tile([P, 4, N], U32, tag="dq", bufs=2, align_bytes=64)
-            ds = work.tile([P, 4, N], U8, tag="ds", bufs=2, align_bytes=64)
-            nc.vector.quantize_mx(
-                out=dq[:, 1:3, :].rearrange("p g n -> p (g n)").bitcast(E5),
-                scales=ds[:, 1:3, :].rearrange("p g n -> p (g n)"),
-                in_=s["dz"][:, 0:2, :].rearrange("p g n -> p (g n)"),
-            )
-            nc.vector.quantize_mx(out=dq[:, 3, :].bitcast(E5), scales=ds[:, 3, :], in_=s["dz"][:, 2, :])
-            nc.vector.quantize_mx(out=dq[:, 0, :].bitcast(E5), scales=ds[:, 0, :], in_=dzf_slice(t))
-            s["dq"] = dq
-            s["ds"] = ds
-
-        def out0_mm(t):
-            s = st[t]
-            s["acc"] = []
-            for m in range(N // P):
-                ps = psum.tile([P, C], F32, tag="mm", bufs=3)
-                ms = slice(m * P, (m + 1) * P)
-                for k, gi in enumerate((1, 2, 3, 0)):
-                    nc.tensor.matmul_mx(
-                        out=ps[:],
-                        lhsT=s["dq"][:, gi, ms].bitcast(E5),
-                        lhsT_scale=s["ds"][:, gi, ms],
-                        rhs=wq[:, gi, :].bitcast(E4),
-                        rhs_scale=ws[:, gi, :],
-                        start=(k == 0),
-                        stop=(k == 3),
-                    )
-                s["acc"].append(ps)
-
-        def out0_evac(t, engs):
-            s = st[t]
-            b, f0 = place(t)
-            for m in range(N // P):
-                o = work.tile([P, C], F32, tag="osb", bufs=4)
-                if engs[m % len(engs)] == "s":
-                    nc.scalar.copy(out=o[:], in_=s["acc"][m][:])
-                else:
-                    nc.vector.tensor_copy(out=o[:], in_=s["acc"][m][:])
-                nc.sync.dma_start(out=out_0[b, f0 + m * P : f0 + (m + 1) * P, :], in_=o[:])
-
-        def hid(g):
+        def hid_tr(g):
             words = half[g]["h"][:].rearrange("p m f -> p (m f)").bitcast(F32)
-            grp = work.tile([P, H, J], BF16, tag="hgrp", bufs=1, align_bytes=64)
-            gw = flat(grp).bitcast(F32).rearrange("p (r u) -> p r u", u=2)
             s0 = (g % 2) * (PASS // 2)
+            half[g]["hp"] = []
             for mm in range(2):
                 ps = psum.tile([P, 2, 2 * P], F32, tag="mm", bufs=3)
                 for m in range(2):
@@ -279,19 +136,33 @@ def tile_batchedlstm_v_kernel(
                         nc.tensor.transpose(
                             ps[:, u, m * P : (m + 1) * P], words[:, w0 + u : w0 + PASS // 2 : 2], ident[:]
                         )
-                nc.scalar.copy(out=gw[:, mm * 2 * P : (mm + 1) * 2 * P, :], in_=ps[:].rearrange("p u r -> p r u"))
+                half[g]["hp"].append(ps)
+
+        def hid_evac(g):
+            grp = work.tile([P, H, J], BF16, tag="hgrp", bufs=1, align_bytes=64)
+            gw = flat(grp).bitcast(F32).rearrange("p (r u) -> p r u", u=2)
+            for mm in range(2):
+                nc.scalar.copy(
+                    out=gw[:, mm * 2 * P : (mm + 1) * 2 * P, :], in_=half[g]["hp"][mm][:].rearrange("p u r -> p r u")
+                )
             half[g]["hg"] = grp
 
         def quant_h(g):
             nc.vector.quantize_mx(out=xq[:, g, 1, :].bitcast(E4), scales=xs[:, g, 1, :], in_=flat(half[g]["hg"]))
 
-        def dft(g, engs):
+        def dft_tr(g):
             words = flat(half[g]["dzf"]).bitcast(F32).rearrange("p (q t w) -> p t w q", t=J, w=2)
-            grp = work.tile([P, 2, 2, P, J], BF16, tag="dft", bufs=1, align_bytes=64)
+            half[g]["fp"] = []
             for w in range(2):
                 ps = psum.tile([P, J, P], F32, tag="mm", bufs=3)
                 for t in range(J):
                     nc.tensor.transpose(ps[:, t, :], words[:, t, w, :], ident[:])
+                half[g]["fp"].append(ps)
+
+        def dft_evac(g, engs):
+            grp = work.tile([P, 2, 2, P, J], BF16, tag="dft", bufs=1, align_bytes=64)
+            for w in range(2):
+                ps = half[g]["fp"][w]
                 src = ps[:].rearrange("p t m -> p (t m)").bitcast(BF16).rearrange("p (t m e) -> p e m t", t=J, e=2)
                 if engs[w] == "s":
                     nc.scalar.copy(out=grp[:, w], in_=src)
@@ -306,114 +177,403 @@ def tile_batchedlstm_v_kernel(
                 in_=half[g]["fg"][:].rearrange("p w e m t -> p (w e m t)"),
             )
 
+        def act_sb(t, gi, nm, fn):
+            s = st[t]
+            v = work.tile([P, s["n"], J], F32, tag=nm, bufs=2)
+            nc.scalar.activation(
+                out=v[:].rearrange("p (c i) j -> p c j i", i=4),
+                in_=s["z" + str(gi)][:].rearrange("p j (c i) -> p c j i", i=4),
+                func=fn,
+            )
+            s[nm] = v
+
+        def acts_g(t):
+            s = st[t]
+            act_sb(t, 2, "g", ACT.Tanh)
+            g2 = work.tile([P, s["n"], J], F32, tag="g2", bufs=2)
+            nc.scalar.activation(out=flat(g2), in_=flat(s["g"]), func=ACT.Square)
+            s["g2"] = g2
+
+        def acts(t):
+            act_sb(t, 0, "f", ACT.Sigmoid)
+            acts_g(t)
+            act_sb(t, 3, "o", ACT.Sigmoid)
+
+        def halves(t):
+            return range(st[t]["n"] // P)
+
+        def zi_tr(t):
+            s = st[t]
+            s["zip"] = []
+            for h in halves(t):
+                ps = psum.tile([P, J, P], F32, tag="mm", bufs=3)
+                for j in range(J):
+                    nc.tensor.transpose(ps[:, j, :], s["z1"][:, j, h * P : (h + 1) * P], ident[:])
+                s["zip"].append(ps)
+
+        def i_act(t):
+            s = st[t]
+            iT = work.tile([P, s["n"] // P, J, P], F32, tag="iT", bufs=1)
+            for h in halves(t):
+                nc.scalar.activation(out=iT[:, h], in_=s["zip"][h][:], func=ACT.Sigmoid)
+            s["iT"] = iT
+
+        def i_back(t):
+            s = st[t]
+            s["i"] = []
+            for h in halves(t):
+                ps = psum.tile([P, J, P], F32, tag="i", bufs=2)
+                for j in range(J):
+                    nc.tensor.transpose(ps[:, j, :], s["iT"][:, h, j, :], ident[:])
+                s["i"].append(ps)
+
+        def i_view(t, h):
+            return st[t]["i"][h][:].rearrange("p j f -> p f j")
+
+        def less_one_times(out, in0, in1):
+            nc.vector.scalar_tensor_tensor(out=out, in0=in0, scalar=1.0, in1=in1, op0=ALU.subtract, op1=ALU.mult)
+
+        def v_a(t):
+            s = st[t]
+            a = work.tile([P, s["n"], J], F32, tag="a", bufs=1)
+            cell = half[s["pa"]]["cell"]
+            nc.vector.tensor_tensor(
+                out=a[:], in0=cell[:, :, s["l"] : s["l"] + s["n"]].rearrange("p j f -> p f j"), in1=s["f"][:], op=ALU.mult
+            )
+            s["a"] = a
+
+        def v_b(t):
+            s = st[t]
+            bb = work.tile([P, s["n"], J], F32, tag="b", bufs=1)
+            for h in halves(t):
+                hs = slice(h * P, (h + 1) * P)
+                nc.vector.tensor_tensor(out=bb[:, hs, :], in0=i_view(t, h), in1=s["g"][:, hs, :], op=ALU.mult)
+            s["b"] = bb
+
+        def v_xi_xg(t):
+            s = st[t]
+            for h in halves(t):
+                hs = slice(h * P, (h + 1) * P)
+                less_one_times(s["g"][:, hs, :], i_view(t, h), s["b"][:, hs, :])
+            for h in halves(t):
+                hs = slice(h * P, (h + 1) * P)
+                less_one_times(s["g2"][:, hs, :], s["g2"][:, hs, :], i_view(t, h))
+
+        def v_xf(t):
+            s = st[t]
+            less_one_times(flat(s["f"]), flat(s["f"]), flat(s["a"]))
+
+        def v_y(t):
+            s = st[t]
+            less_one_times(flat(s["o"]), flat(s["o"]), flat(s["go"]))
+
+        def c_th(t):
+            s = st[t]
+            n = s["n"]
+            th = work.tile([P, n * J], F32, tag="thT", bufs=1)
+            sq = work.tile([P, n * J], F32, tag="sqT", bufs=1)
+            for h in halves(t):
+                ps = psum.tile([P, 512], F32, tag="mm", bufs=3)
+                for k in range(4):
+                    cols = slice(h * 512 + k * P, h * 512 + (k + 1) * P)
+                    dst = ps[:, k * P : (k + 1) * P]
+                    nc.tensor.matmul(
+                        out=dst, lhsT=flat(s["a"])[:, cols], rhs=ident[:], is_transpose=True, start=True, stop=False
+                    )
+                    nc.tensor.matmul(
+                        out=dst, lhsT=flat(s["b"])[:, cols], rhs=ident[:], is_transpose=True, start=False, stop=True
+                    )
+                nc.scalar.activation(out=th[:, h * 512 : (h + 1) * 512], in_=ps[:], func=ACT.Tanh, scale=-1.0)
+            nc.scalar.activation(out=sq[:], in_=th[:], func=ACT.Square)
+            s["thT"] = th
+            s["sqT"] = sq
+
+        def back(t, nm):
+            s = st[t]
+            s[nm] = []
+            for h in halves(t):
+                ps = psum.tile([P, 512], F32, tag="bk", bufs=2)
+                for k in range(4):
+                    c0 = h * 512 + k * P
+                    nc.tensor.transpose(ps[:, k * P : (k + 1) * P], s[nm + "T"][:, c0 : c0 + P], ident[:])
+                s[nm].append(ps)
+
+        def gh(t):
+            s = st[t]
+            n = s["n"]
+            ps = psum.tile([P, 2, n], F32, tag="gh", bufs=1)
+            words = half[s["pa"]]["gout"][:].rearrange("p m h -> p (m h)").bitcast(F32)
+            m0 = s["l"] // P
+            for m in range(n // P):
+                for u in range(2):
+                    w0 = (m0 + m) * (H // 2) + u
+                    nc.tensor.transpose(
+                        ps[:, u, m * P : (m + 1) * P], words[:, w0 : (m0 + m + 1) * (H // 2) : 2], ident[:]
+                    )
+            s["gh"] = ps
+
+        def v_go(t):
+            s = st[t]
+            go = work.tile([P, s["n"], J], F32, tag="go", bufs=2)
+            nc.vector.tensor_tensor(
+                out=go[:].rearrange("p f (u e) -> p f u e", e=2),
+                in0=s["gh"][:].rearrange("p u f -> p (u f)").bitcast(BF16).rearrange("p (u f e) -> p f u e", u=2, e=2),
+                in1=s["o"][:].rearrange("p f (u e) -> p f u e", e=2),
+                op=ALU.mult,
+            )
+            s["go"] = go
+
+        def v_ndc(t):
+            s = st[t]
+            n = s["n"]
+            ndc = work.tile([P, n, J], F32, tag="ndc", bufs=1)
+            for h in halves(t):
+                hs = slice(h * 512, (h + 1) * 512)
+                less_one_times(flat(ndc)[:, hs], s["sq"][h][:], flat(s["go"])[:, hs])
+            s["ndc"] = ndc
+            if s["l"] == 0:
+                dzf = work.tile([P, PASS, J], BF16, tag="dzf", bufs=2, align_bytes=64)
+                half[s["pa"]]["dzf"] = dzf
+            dz = work.tile([P, 3, n * J], BF16, tag="dz", bufs=2, align_bytes=64)
+            s["dz"] = dz
+
+        def dzf_slice(t):
+            s = st[t]
+            return flat(half[s["pa"]]["dzf"])[:, s["l"] * J : (s["l"] + s["n"]) * J]
+
+        def dz_f(t, eng):
+            s = st[t]
+            for h in halves(t):
+                hs = slice(h * 512, (h + 1) * 512)
+                eng.tensor_tensor(out=dzf_slice(t)[:, hs], in0=flat(s["f"])[:, hs], in1=flat(s["ndc"])[:, hs], op=ALU.mult)
+
+        def dz_i(t, eng):
+            s = st[t]
+            eng.tensor_tensor(out=s["dz"][:, 0, :], in0=flat(s["g"]), in1=flat(s["ndc"]), op=ALU.mult)
+
+        def dz_g(t, eng, lo=0, hi=2):
+            s = st[t]
+            q = slice(lo * s["n"] * J // 2, hi * s["n"] * J // 2)
+            eng.tensor_tensor(out=s["dz"][:, 1, q], in0=flat(s["g2"])[:, q], in1=flat(s["ndc"])[:, q], op=ALU.mult)
+
+        def dz_o(t):
+            s = st[t]
+            for h in halves(t):
+                hs = slice(h * 512, (h + 1) * 512)
+                nc.vector.tensor_tensor(
+                    out=s["dz"][:, 2, hs], in0=s["th"][h][:], in1=flat(s["o"])[:, hs], op=ALU.mult
+                )
+
+        def quants(t):
+            s = st[t]
+            n = s["n"]
+            dq = work.tile([P, 4, n], U32, tag="dq", bufs=2, align_bytes=64)
+            ds = work.tile([P, 4, n], U8, tag="ds", bufs=2, align_bytes=64)
+            nc.vector.quantize_mx(out=dq[:, 0, :].bitcast(E5), scales=ds[:, 0, :], in_=dzf_slice(t))
+            nc.vector.quantize_mx(out=dq[:, 3, :].bitcast(E5), scales=ds[:, 3, :], in_=s["dz"][:, 2, :])
+            nc.vector.quantize_mx(
+                out=dq[:, 1:3, :].rearrange("p g n -> p (g n)").bitcast(E5),
+                scales=ds[:, 1:3, :].rearrange("p g n -> p (g n)"),
+                in_=s["dz"][:, 0:2, :].rearrange("p g n -> p (g n)"),
+            )
+            s["dq"] = dq
+            s["ds"] = ds
+
+        def out0_mm(t):
+            s = st[t]
+            s["acc"] = []
+            for m in halves(t):
+                ps = psum.tile([P, C], F32, tag="mm", bufs=3)
+                ms = slice(m * P, (m + 1) * P)
+                for k, gi in enumerate((0, 3, 1, 2)):
+                    nc.tensor.matmul_mx(
+                        out=ps[:],
+                        lhsT=s["dq"][:, gi, ms].bitcast(E5),
+                        lhsT_scale=s["ds"][:, gi, ms],
+                        rhs=wq[:, gi, :].bitcast(E4),
+                        rhs_scale=ws[:, gi, :],
+                        start=(k == 0),
+                        stop=(k == 3),
+                    )
+                s["acc"].append(ps)
+
+        def out0_evac(t, engs):
+            s = st[t]
+            b, f0 = divmod(s["tok"], F)
+            for m in halves(t):
+                o = work.tile([P, C], F32, tag="osb", bufs=4)
+                if engs[m % len(engs)] == "s":
+                    nc.scalar.copy(out=o[:], in_=s["acc"][m][:])
+                else:
+                    nc.vector.tensor_copy(out=o[:], in_=s["acc"][m][:])
+                nc.sync.dma_start(out=out_0[b, f0 + m * P : f0 + (m + 1) * P, :], in_=o[:])
+
         out1_view = out_1.rearrange("(m j) k -> j m k", j=J)
 
-        def out1(j, kh, tag, bufs, eng):
-            ps = psum.tile([P, 512], F32, tag=tag, bufs=bufs)
+        def out1_mm(ps, j, kh, g0, g1, first, final):
             js = slice(j * P, (j + 1) * P)
-            for g in range(4):
+            for g in range(g0, g1):
                 nc.tensor.matmul_mx(
                     out=ps[:],
                     lhsT=fq[:, g, js].bitcast(E5),
                     lhsT_scale=fs[:, g, js],
                     rhs=xq[:, g, kh, :].bitcast(E4),
                     rhs_scale=xs[:, g, kh, :],
-                    start=(g == 0),
-                    stop=(g == 3),
+                    start=(g == first),
+                    stop=(g == final),
                 )
-            o = work.tile([P, C], F32, tag="osb", bufs=4)
-            if eng == "s":
-                nc.scalar.copy(out=o[:], in_=ps[:])
-            else:
-                nc.vector.tensor_copy(out=o[:], in_=ps[:])
-            nc.sync.dma_start(out=out1_view[j][:, kh * 512 : (kh + 1) * 512], in_=o[:])
 
-        for unused in range(1):
+        parts = []
+
+        def out1_part_mm(k):
+            if k % 2 == 0:
+                tile = work.tile([P, 2, 512], F32, tag=("raw", "grp")[k // 2 % 2], bufs=2, align_bytes=64)
+                parts.append(tile[:, 0, :])
+                parts.append(tile[:, 1, :])
+            ps = psum.tile([P, 512], F32, tag="mm", bufs=3)
+            out1_mm(ps, k % 4, k // 4, 0, 2, 0, 1)
+            half[k % 4]["pp" + str(k // 4)] = ps
+
+        def out1_part_evac(k):
+            nc.scalar.copy(out=parts[k], in_=half[k % 4]["pp" + str(k // 4)][:])
+
+        def out1_final(ps, k):
+            o = work.tile([P, C], F32, tag="z" + str(k % 4), bufs=2)
+            nc.vector.tensor_tensor(out=o[:], in0=ps[:], in1=parts[k], op=ALU.add)
+            nc.sync.dma_start(out=out1_view[k % 4][:, k // 4 * 512 : (k // 4 + 1) * 512], in_=o[:])
+
+        s_jobs = {}
+        v_jobs = {}
+        p_jobs = {}
+        l_jobs = {}
+
+        def add(dct, t, fn):
+            dct.setdefault(t, []).append(fn)
+
+        add(v_jobs, 0, lambda: quant_w(0))
+        add(v_jobs, 0, lambda: quant_w(1))
+        add(v_jobs, 0, lambda: ilv_w(2, "v"))
+        add(v_jobs, 0, lambda: ilv_w(3, "v"))
+        add(v_jobs, 0, lambda: quant_w(2))
+        add(v_jobs, 1, lambda: quant_w(3))
+        for g in range(4):
+            it = X_AT[g]
+            add(l_jobs, it - 1, lambda g=g: load_x(g))
+            add(s_jobs, it, lambda g=g: ilv_x(g, "s"))
+            add(v_jobs, it + 1, lambda g=g: quant_x(g))
+            ih = H_AT[g]
+            if g % 2 == 0:
+                add(l_jobs, ih - 1, lambda g=g: load_hidden(g // 2))
+            add(p_jobs, ih, lambda g=g: hid_tr(g))
+            add(s_jobs, ih, lambda g=g: hid_evac(g))
+            add(v_jobs, ih + 1, lambda g=g: quant_h(g))
+        for g in range(3):
+            tl = max(t for t in range(TILES) if st[t]["pa"] == g)
+            add(p_jobs, tl + 1, lambda g=g: dft_tr(g))
+            add(s_jobs, tl + 1, lambda g=g: dft_evac(g, "ss"))
+            add(v_jobs, tl + 2, lambda g=g: quant_ft(g))
+
+        for k in range(8):
+            add(p_jobs, PART_AT[k], lambda k=k: out1_part_mm(k))
+            add(s_jobs, PART_AT[k], lambda k=k: out1_part_evac(k))
+
+        def run(dct, t):
+            for fn in dct.get(t, []):
+                fn()
+
+        with tc.manual_schedule(engines={ENG.PE, ENG.Activation, ENG.DVE, ENG.Pool}):
             load_gate(0, 0)
-            load_half(0)
             load_gate(0, 1)
+            load_half(0, (0, 1))
             load_gate(0, 2)
             load_gate(0, 3)
             load_w(0)
             load_w(1)
-            for gi in range(4):
+            for gi in (0, 1, 2, 3):
                 load_gate(1, gi)
+            load_half(0, (1, 4))
             load_w(2)
             load_w(3)
-            acts(0)
+            zi_tr(0)
+            i_act(0)
+            i_back(0)
             gh(0)
-            half[0]["wg"] = interleave("v", half[0]["w"])
+            acts(0)
+            v_a(0)
+            ilv_w(0, "v")
+            ilv_w(1, "v")
 
-            for t in range(TILES + 1):
-                last = t == TILES
+            for t in range(TILES):
                 if t + 2 < TILES:
-                    for gi in range(4):
+                    if st[t + 2]["l"] == 0:
+                        load_half(st[t + 2]["pa"], (0, 4))
+                    for gi in (0, 1, 2, 3):
                         load_gate(t + 2, gi)
-                    if (t + 2) % PER_PASS == 0:
-                        load_half((t + 2) // PER_PASS)
-                if 1 <= t <= 4:
-                    load_x(t - 1)
-                if t in (1, 4):
-                    load_hidden((t - 1) // 3)
-
-                if not last:
-                    va(t)
-                    cT(t)
-                if t == 0:
-                    half[1]["wg"] = interleave("v", half[1]["w"])
-                    quant_w(0)
+                run(l_jobs, t)
                 if t > 0:
-                    b_ndc(t - 1)
-                    p = st[t - 1]
-                    if last:
-                        nc.vector.tensor_tensor(out=dzf_slice(t - 1), in0=flat(p["f"]), in1=flat(p["ndc"]), op=ALU.mult)
-                    else:
-                        nc.gpsimd.tensor_tensor(out=dzf_slice(t - 1), in0=flat(p["f"]), in1=flat(p["ndc"]), op=ALU.mult)
-                    b_o(t - 1)
-                if not last:
-                    vgo(t)
+                    v_ndc(t - 1)
+                    dz_f(t - 1, nc.gpsimd)
+                    dz_i(t - 1, nc.gpsimd)
+                    dz_g(t - 1, nc.gpsimd, 0, 1)
+                    back(t - 1, "th")
+                v_b(t)
+                c_th(t)
+                v_xi_xg(t)
                 if t > 0:
-                    nc.vector.tensor_tensor(out=p["dz"][:, 0, :], in0=flat(p["g"]), in1=flat(p["ndc"]), op=ALU.mult)
-                    nc.vector.tensor_tensor(out=p["dz"][:, 1, :], in0=flat(p["i"]), in1=flat(p["ndc"]), op=ALU.mult)
-                if not last:
-                    s = st[t]
-                    minus_one_times(flat(s["f"]), flat(s["f"]), flat(s["a"]))
-                if t == 0:
-                    quant_w(1)
-                if t == 1:
-                    quant_w(2)
-                    quant_w(3)
-                if last:
-                    dft(3, "sv")
-                    quant_ft(3)
+                    dz_o(t - 1)
+                v_go(t)
+                if t > 0:
+                    dz_g(t - 1, nc.vector, 1, 2)
+                v_xf(t)
+                v_y(t)
+                if t + 1 < TILES:
+                    zi_tr(t + 1)
+                    i_act(t + 1)
+                    act_sb(t + 1, 0, "f", ACT.Sigmoid)
+                    acts_g(t + 1)
+                if t > 1:
+                    out0_mm(t - 2)
+                    out0_evac(t - 2, "s")
+                if t + 1 < TILES:
+                    i_back(t + 1)
+                    act_sb(t + 1, 3, "o", ACT.Sigmoid)
+                    gh(t + 1)
+                back(t, "sq")
+                run(p_jobs, t)
+                run(s_jobs, t)
                 if t > 0:
                     quants(t - 1)
-                if not last:
-                    minus_one_times(flat(s["g"]), flat(s["i"]), flat(s["b"]))
-                    minus_one_times(flat(s["i"]), flat(s["g2"]), flat(s["i"]))
-                    minus_one_times(flat(s["o"]), flat(s["o"]), flat(s["go"]))
+                run(v_jobs, t)
                 if t + 1 < TILES:
-                    acts(t + 1)
-                    gh(t + 1)
-                if t == 0:
-                    half[2]["wg"] = interleave("s", half[2]["w"])
-                    half[3]["wg"] = interleave("s", half[3]["w"])
-                if not last and t > 0:
-                    if t % PER_PASS == 0:
-                        dft(t // PER_PASS - 1, "ss")
-                        quant_ft(t // PER_PASS - 1)
-                    if 2 <= t <= 5:
-                        half[t - 2]["xg"] = interleave("s", half[t - 2]["x"])
-                        quant_x(t - 2)
-                    if t in (2, 3, 5, 6):
-                        g = {2: 0, 3: 1, 5: 2, 6: 3}[t]
-                        hid(g)
-                        quant_h(g)
-                    out0_mm(t - 1)
-                    out0_evac(t - 1, "s")
-                if not last:
-                    back(t)
-            out0_mm(TILES - 1)
-            out0_evac(TILES - 1, "vs")
+                    v_a(t + 1)
+
+            t = TILES
+            v_ndc(t - 1)
+            dz_f(t - 1, nc.vector)
+            back(t - 1, "th")
+            dft_tr(3)
+            dft_evac(3, "ss")
+            out0_mm(t - 2)
+            out0_evac(t - 2, "s")
+            dz_o(t - 1)
+            dz_i(t - 1, nc.vector)
+            dz_g(t - 1, nc.vector)
+            tags = [("i", 2), ("i", 2), ("gh", 1), ("bk", 2), ("bk", 2), ("mm", 3), ("mm", 3), ("mm", 3)]
+            banks = []
+            for k in range(5):
+                ps = psum.tile([P, 512], F32, tag=tags[k][0], bufs=tags[k][1])
+                out1_mm(ps, k % 4, k // 4, 2, 3, 2, 3)
+                banks.append(ps)
+            run(v_jobs, t)
+            quants(t - 1)
+            out0_mm(t - 1)
+            out0_evac(t - 1, "s")
+            quant_ft(3)
             for k in range(8):
-                out1(k % 4, k // 4, "bk", 4, "sv"[k % 2])
+                if k < 5:
+                    out1_mm(banks[k], k % 4, k // 4, 3, 4, 2, 3)
+                    ps = banks[k]
+                else:
+                    ps = psum.tile([P, 512], F32, tag=tags[k][0], bufs=tags[k][1])
+                    out1_mm(ps, k % 4, k // 4, 2, 4, 2, 3)
+                out1_final(ps, k)

from contextlib import ExitStack

import concourse.mybir as mybir
from concourse.masks import make_identity

F32 = mybir.dt.float32
BF16 = mybir.dt.bfloat16
U32 = mybir.dt.uint32
U8 = mybir.dt.uint8
E4 = mybir.dt.float8_e4m3fn_x4
E5 = mybir.dt.float8_e5m2_x4
ALU = mybir.AluOpType
ACT = mybir.ActivationFunctionType
ENG = mybir.EngineType

B, F, C, H = 2, 1024, 512, 512
T = B * F
P = 128
J = 4
PASS = P * J

FLOPS = 2 * T * (4 * H) * C + 2 * H * T * (C + H)
BYTES = 4 * B * 4 * H * F + 2 * (4 * B * F * H + 4 * H * C) + 4 * (T * C + H * (C + H))

SIZES = [128, 128, 256, 256, 256, 256, 256, 256, 128, 128]
STARTS = [sum(SIZES[:k]) for k in range(len(SIZES))]
TILES = len(SIZES)
X_AT = [2, 3, 4, 5]
H_AT = [2, 3, 5, 6]
PART_AT = [7, 7, 7, 8, 8, 8, 9, 9]


def tile_batchedlstm_v_kernel(
    tc, x, hidden_state, cell_state, W_f, b_f, W_i, b_i, W_o, b_o, W_g, b_g, gates, grad_out, out_0, out_1
):
    nc = tc.nc
    weights = [W_f, W_i, W_g, W_o]

    with ExitStack() as ctx:
        keep = ctx.enter_context(tc.tile_pool(name="keep", bufs=1))
        work = ctx.enter_context(tc.tile_pool(name="work", bufs=2))
        psum = ctx.enter_context(tc.psum_pool(name="psum", bufs=1))

        ident = keep.tile([P, P], F32, tag="ident")
        wq = keep.tile([P, 4, C], U32, tag="wq", align_bytes=64)
        ws = keep.tile([P, 4, C], U8, tag="ws", align_bytes=64)
        xq = keep.tile([P, 4, 2, 512], U32, tag="xq", align_bytes=64)
        xs = keep.tile([P, 4, 2, 512], U8, tag="xs", align_bytes=64)
        fq = keep.tile([P, 4, H], U32, tag="fq", align_bytes=64)
        fs = keep.tile([P, 4, H], U8, tag="fs", align_bytes=64)
        warm = keep.tile([P, 8], F32, tag="warm")

        make_identity(nc, ident[:])
        nc.vector.memset(warm[:], 0.0)
        nc.scalar.activation(out=warm[:], in_=warm[:], func=ACT.Sigmoid)

        st = [dict(n=SIZES[t], tok=STARTS[t], pa=STARTS[t] // PASS, l=STARTS[t] % PASS) for t in range(TILES)]
        half = [dict() for g in range(4)]

        def flat(t3):
            return t3[:].rearrange("p c j -> p (c j)")

        def load_half(g, parts):
            b, f0 = divmod(g * PASS, F)
            if "cell" not in half[g]:
                cell = work.tile([P, J, PASS], BF16, tag="cell", bufs=2)
                go = work.tile([P, 4, H], BF16, tag="gout", bufs=2)
                half[g]["cell"] = cell
                half[g]["gout"] = go
            m0, m1 = parts
            nc.sync.dma_start(
                out=half[g]["cell"][:, :, m0 * P : m1 * P],
                in_=cell_state[b].rearrange("(p j) f -> p j f", j=J)[:, :, f0 + m0 * P : f0 + m1 * P],
            )
            nc.sync.dma_start(
                out=half[g]["gout"][:, m0:m1, :],
                in_=grad_out[b, f0 + m0 * P : f0 + m1 * P, :].rearrange("(m p) h -> p m h", p=P),
            )

        def load_gate(t, gi):
            n = st[t]["n"]
            b, f0 = divmod(st[t]["tok"], F)
            z = work.tile([P, J, n], F32, tag="z" + str(gi), bufs=2)
            src = gates[b, gi * H : (gi + 1) * H, f0 : f0 + n].rearrange("(p j) f -> p j f", j=J)
            nc.sync.dma_start(out=z[:], in_=src)
            st[t]["z" + str(gi)] = z

        def load_w(gi):
            raw = work.tile([P, J, C], BF16, tag="raw", bufs=2, align_bytes=64)
            nc.sync.dma_start(out=raw[:], in_=weights[gi][:, 0:C].rearrange("(p j) c -> p j c", j=J))
            half[gi]["w"] = raw

        def load_x(g):
            b, f0 = divmod(g * PASS, F)
            raw = work.tile([P, J, C], BF16, tag="raw", bufs=2, align_bytes=64)
            nc.sync.dma_start(out=raw[:], in_=x[b, f0 : f0 + PASS, :].rearrange("(p j) c -> p j c", j=J))
            half[g]["x"] = raw

        def load_hidden(b):
            raw = work.tile([P, 4, F], BF16, tag="hraw", bufs=1)
            nc.sync.dma_start(out=raw[:], in_=hidden_state[b].rearrange("(m p) f -> p m f", p=P))
            half[2 * b]["h"] = raw
            half[2 * b + 1]["h"] = raw

        def interleave(eng, raw):
            grp = work.tile([P, C, J], BF16, tag="grp", bufs=2, align_bytes=64)
            dst = grp[:].rearrange("p (c i) j -> p c j i", i=4)
            src = raw[:].rearrange("p j (c i) -> p c j i", i=4)
            if eng == "v":
                nc.vector.tensor_copy(out=dst, in_=src)
            else:
                nc.scalar.copy(out=dst, in_=src)
            return grp

        def ilv_w(gi, eng):
            half[gi]["wg"] = interleave(eng, half[gi]["w"])

        def quant_w(gi):
            nc.vector.quantize_mx(out=wq[:, gi, :].bitcast(E4), scales=ws[:, gi, :], in_=flat(half[gi]["wg"]))

        def ilv_x(g, eng):
            half[g]["xg"] = interleave(eng, half[g]["x"])

        def quant_x(g):
            nc.vector.quantize_mx(out=xq[:, g, 0, :].bitcast(E4), scales=xs[:, g, 0, :], in_=flat(half[g]["xg"]))

        def hid_tr(g):
            words = half[g]["h"][:].rearrange("p m f -> p (m f)").bitcast(F32)
            s0 = (g % 2) * (PASS // 2)
            half[g]["hp"] = []
            for mm in range(2):
                ps = psum.tile([P, 2, 2 * P], F32, tag="mm", bufs=3)
                for m in range(2):
                    for u in range(2):
                        w0 = (2 * mm + m) * (F // 2) + s0
                        nc.tensor.transpose(
                            ps[:, u, m * P : (m + 1) * P], words[:, w0 + u : w0 + PASS // 2 : 2], ident[:]
                        )
                half[g]["hp"].append(ps)

        def hid_evac(g):
            grp = work.tile([P, H, J], BF16, tag="hgrp", bufs=1, align_bytes=64)
            gw = flat(grp).bitcast(F32).rearrange("p (r u) -> p r u", u=2)
            for mm in range(2):
                nc.scalar.copy(
                    out=gw[:, mm * 2 * P : (mm + 1) * 2 * P, :], in_=half[g]["hp"][mm][:].rearrange("p u r -> p r u")
                )
            half[g]["hg"] = grp

        def quant_h(g):
            nc.vector.quantize_mx(out=xq[:, g, 1, :].bitcast(E4), scales=xs[:, g, 1, :], in_=flat(half[g]["hg"]))

        def dft_tr(g):
            words = flat(half[g]["dzf"]).bitcast(F32).rearrange("p (q t w) -> p t w q", t=J, w=2)
            half[g]["fp"] = []
            for w in range(2):
                ps = psum.tile([P, J, P], F32, tag="mm", bufs=3)
                for t in range(J):
                    nc.tensor.transpose(ps[:, t, :], words[:, t, w, :], ident[:])
                half[g]["fp"].append(ps)

        def dft_evac(g, engs):
            grp = work.tile([P, 2, 2, P, J], BF16, tag="dft", bufs=1, align_bytes=64)
            for w in range(2):
                ps = half[g]["fp"][w]
                src = ps[:].rearrange("p t m -> p (t m)").bitcast(BF16).rearrange("p (t m e) -> p e m t", t=J, e=2)
                if engs[w] == "s":
                    nc.scalar.copy(out=grp[:, w], in_=src)
                else:
                    nc.vector.tensor_copy(out=grp[:, w], in_=src)
            half[g]["fg"] = grp

        def quant_ft(g):
            nc.vector.quantize_mx(
                out=fq[:, g, :].bitcast(E5),
                scales=fs[:, g, :],
                in_=half[g]["fg"][:].rearrange("p w e m t -> p (w e m t)"),
            )

        def act_sb(t, gi, nm, fn):
            s = st[t]
            v = work.tile([P, s["n"], J], F32, tag=nm, bufs=2)
            nc.scalar.activation(
                out=v[:].rearrange("p (c i) j -> p c j i", i=4),
                in_=s["z" + str(gi)][:].rearrange("p j (c i) -> p c j i", i=4),
                func=fn,
            )
            s[nm] = v

        def acts_g(t):
            s = st[t]
            act_sb(t, 2, "g", ACT.Tanh)
            g2 = work.tile([P, s["n"], J], F32, tag="g2", bufs=2)
            nc.scalar.activation(out=flat(g2), in_=flat(s["g"]), func=ACT.Square)
            s["g2"] = g2

        def acts(t):
            act_sb(t, 0, "f", ACT.Sigmoid)
            acts_g(t)
            act_sb(t, 3, "o", ACT.Sigmoid)

        def halves(t):
            return range(st[t]["n"] // P)

        def zi_tr(t):
            s = st[t]
            s["zip"] = []
            for h in halves(t):
                ps = psum.tile([P, J, P], F32, tag="mm", bufs=3)
                for j in range(J):
                    nc.tensor.transpose(ps[:, j, :], s["z1"][:, j, h * P : (h + 1) * P], ident[:])
                s["zip"].append(ps)

        def i_act(t):
            s = st[t]
            iT = work.tile([P, s["n"] // P, J, P], F32, tag="iT", bufs=1)
            for h in halves(t):
                nc.scalar.activation(out=iT[:, h], in_=s["zip"][h][:], func=ACT.Sigmoid)
            s["iT"] = iT

        def i_back(t):
            s = st[t]
            s["i"] = []
            for h in halves(t):
                ps = psum.tile([P, J, P], F32, tag="i", bufs=2)
                for j in range(J):
                    nc.tensor.transpose(ps[:, j, :], s["iT"][:, h, j, :], ident[:])
                s["i"].append(ps)

        def i_view(t, h):
            return st[t]["i"][h][:].rearrange("p j f -> p f j")

        def less_one_times(out, in0, in1):
            nc.vector.scalar_tensor_tensor(out=out, in0=in0, scalar=1.0, in1=in1, op0=ALU.subtract, op1=ALU.mult)

        def v_a(t):
            s = st[t]
            a = work.tile([P, s["n"], J], F32, tag="a", bufs=1)
            cell = half[s["pa"]]["cell"]
            nc.vector.tensor_tensor(
                out=a[:], in0=cell[:, :, s["l"] : s["l"] + s["n"]].rearrange("p j f -> p f j"), in1=s["f"][:], op=ALU.mult
            )
            s["a"] = a

        def v_b(t):
            s = st[t]
            bb = work.tile([P, s["n"], J], F32, tag="b", bufs=1)
            for h in halves(t):
                hs = slice(h * P, (h + 1) * P)
                nc.vector.tensor_tensor(out=bb[:, hs, :], in0=i_view(t, h), in1=s["g"][:, hs, :], op=ALU.mult)
            s["b"] = bb

        def v_xi_xg(t):
            s = st[t]
            for h in halves(t):
                hs = slice(h * P, (h + 1) * P)
                less_one_times(s["g"][:, hs, :], i_view(t, h), s["b"][:, hs, :])
            for h in halves(t):
                hs = slice(h * P, (h + 1) * P)
                less_one_times(s["g2"][:, hs, :], s["g2"][:, hs, :], i_view(t, h))

        def v_xf(t):
            s = st[t]
            less_one_times(flat(s["f"]), flat(s["f"]), flat(s["a"]))

        def v_y(t):
            s = st[t]
            less_one_times(flat(s["o"]), flat(s["o"]), flat(s["go"]))

        def c_th(t):
            s = st[t]
            n = s["n"]
            th = work.tile([P, n * J], F32, tag="thT", bufs=1)
            sq = work.tile([P, n * J], F32, tag="sqT", bufs=1)
            for h in halves(t):
                ps = psum.tile([P, 512], F32, tag="mm", bufs=3)
                for k in range(4):
                    cols = slice(h * 512 + k * P, h * 512 + (k + 1) * P)
                    dst = ps[:, k * P : (k + 1) * P]
                    nc.tensor.matmul(
                        out=dst, lhsT=flat(s["a"])[:, cols], rhs=ident[:], is_transpose=True, start=True, stop=False
                    )
                    nc.tensor.matmul(
                        out=dst, lhsT=flat(s["b"])[:, cols], rhs=ident[:], is_transpose=True, start=False, stop=True
                    )
                nc.scalar.activation(out=th[:, h * 512 : (h + 1) * 512], in_=ps[:], func=ACT.Tanh, scale=-1.0)
            nc.scalar.activation(out=sq[:], in_=th[:], func=ACT.Square)
            s["thT"] = th
            s["sqT"] = sq

        def back(t, nm):
            s = st[t]
            s[nm] = []
            for h in halves(t):
                ps = psum.tile([P, 512], F32, tag="bk", bufs=2)
                for k in range(4):
                    c0 = h * 512 + k * P
                    nc.tensor.transpose(ps[:, k * P : (k + 1) * P], s[nm + "T"][:, c0 : c0 + P], ident[:])
                s[nm].append(ps)

        def gh(t):
            s = st[t]
            n = s["n"]
            ps = psum.tile([P, 2, n], F32, tag="gh", bufs=1)
            words = half[s["pa"]]["gout"][:].rearrange("p m h -> p (m h)").bitcast(F32)
            m0 = s["l"] // P
            for m in range(n // P):
                for u in range(2):
                    w0 = (m0 + m) * (H // 2) + u
                    nc.tensor.transpose(
                        ps[:, u, m * P : (m + 1) * P], words[:, w0 : (m0 + m + 1) * (H // 2) : 2], ident[:]
                    )
            s["gh"] = ps

        def v_go(t):
            s = st[t]
            go = work.tile([P, s["n"], J], F32, tag="go", bufs=2)
            nc.vector.tensor_tensor(
                out=go[:].rearrange("p f (u e) -> p f u e", e=2),
                in0=s["gh"][:].rearrange("p u f -> p (u f)").bitcast(BF16).rearrange("p (u f e) -> p f u e", u=2, e=2),
                in1=s["o"][:].rearrange("p f (u e) -> p f u e", e=2),
                op=ALU.mult,
            )
            s["go"] = go

        def v_ndc(t):
            s = st[t]
            n = s["n"]
            ndc = work.tile([P, n, J], F32, tag="ndc", bufs=1)
            for h in halves(t):
                hs = slice(h * 512, (h + 1) * 512)
                less_one_times(flat(ndc)[:, hs], s["sq"][h][:], flat(s["go"])[:, hs])
            s["ndc"] = ndc
            if s["l"] == 0:
                dzf = work.tile([P, PASS, J], BF16, tag="dzf", bufs=2, align_bytes=64)
                half[s["pa"]]["dzf"] = dzf
            dz = work.tile([P, 3, n * J], BF16, tag="dz", bufs=2, align_bytes=64)
            s["dz"] = dz

        def dzf_slice(t):
            s = st[t]
            return flat(half[s["pa"]]["dzf"])[:, s["l"] * J : (s["l"] + s["n"]) * J]

        def dz_f(t, eng):
            s = st[t]
            for h in halves(t):
                hs = slice(h * 512, (h + 1) * 512)
                eng.tensor_tensor(out=dzf_slice(t)[:, hs], in0=flat(s["f"])[:, hs], in1=flat(s["ndc"])[:, hs], op=ALU.mult)

        def dz_i(t, eng):
            s = st[t]
            eng.tensor_tensor(out=s["dz"][:, 0, :], in0=flat(s["g"]), in1=flat(s["ndc"]), op=ALU.mult)

        def dz_g(t, eng, lo=0, hi=2):
            s = st[t]
            q = slice(lo * s["n"] * J // 2, hi * s["n"] * J // 2)
            eng.tensor_tensor(out=s["dz"][:, 1, q], in0=flat(s["g2"])[:, q], in1=flat(s["ndc"])[:, q], op=ALU.mult)

        def dz_o(t):
            s = st[t]
            for h in halves(t):
                hs = slice(h * 512, (h + 1) * 512)
                nc.vector.tensor_tensor(
                    out=s["dz"][:, 2, hs], in0=s["th"][h][:], in1=flat(s["o"])[:, hs], op=ALU.mult
                )

        def quants(t):
            s = st[t]
            n = s["n"]
            dq = work.tile([P, 4, n], U32, tag="dq", bufs=2, align_bytes=64)
            ds = work.tile([P, 4, n], U8, tag="ds", bufs=2, align_bytes=64)
            nc.vector.quantize_mx(out=dq[:, 0, :].bitcast(E5), scales=ds[:, 0, :], in_=dzf_slice(t))
            nc.vector.quantize_mx(out=dq[:, 3, :].bitcast(E5), scales=ds[:, 3, :], in_=s["dz"][:, 2, :])
            nc.vector.quantize_mx(
                out=dq[:, 1:3, :].rearrange("p g n -> p (g n)").bitcast(E5),
                scales=ds[:, 1:3, :].rearrange("p g n -> p (g n)"),
                in_=s["dz"][:, 0:2, :].rearrange("p g n -> p (g n)"),
            )
            s["dq"] = dq
            s["ds"] = ds

        def out0_mm(t):
            s = st[t]
            s["acc"] = []
            for m in halves(t):
                ps = psum.tile([P, C], F32, tag="mm", bufs=3)
                ms = slice(m * P, (m + 1) * P)
                for k, gi in enumerate((0, 3, 1, 2)):
                    nc.tensor.matmul_mx(
                        out=ps[:],
                        lhsT=s["dq"][:, gi, ms].bitcast(E5),
                        lhsT_scale=s["ds"][:, gi, ms],
                        rhs=wq[:, gi, :].bitcast(E4),
                        rhs_scale=ws[:, gi, :],
                        start=(k == 0),
                        stop=(k == 3),
                    )
                s["acc"].append(ps)

        def out0_evac(t, engs):
            s = st[t]
            b, f0 = divmod(s["tok"], F)
            for m in halves(t):
                o = work.tile([P, C], F32, tag="osb", bufs=4)
                if engs[m % len(engs)] == "s":
                    nc.scalar.copy(out=o[:], in_=s["acc"][m][:])
                else:
                    nc.vector.tensor_copy(out=o[:], in_=s["acc"][m][:])
                nc.sync.dma_start(out=out_0[b, f0 + m * P : f0 + (m + 1) * P, :], in_=o[:])

        out1_view = out_1.rearrange("(m j) k -> j m k", j=J)

        def out1_mm(ps, j, kh, g0, g1, first, final):
            js = slice(j * P, (j + 1) * P)
            for g in range(g0, g1):
                nc.tensor.matmul_mx(
                    out=ps[:],
                    lhsT=fq[:, g, js].bitcast(E5),
                    lhsT_scale=fs[:, g, js],
                    rhs=xq[:, g, kh, :].bitcast(E4),
                    rhs_scale=xs[:, g, kh, :],
                    start=(g == first),
                    stop=(g == final),
                )

        parts = []

        def out1_part_mm(k):
            if k % 2 == 0:
                tile = work.tile([P, 2, 512], F32, tag=("raw", "grp")[k // 2 % 2], bufs=2, align_bytes=64)
                parts.append(tile[:, 0, :])
                parts.append(tile[:, 1, :])
            ps = psum.tile([P, 512], F32, tag="mm", bufs=3)
            out1_mm(ps, k % 4, k // 4, 0, 2, 0, 1)
            half[k % 4]["pp" + str(k // 4)] = ps

        def out1_part_evac(k):
            nc.scalar.copy(out=parts[k], in_=half[k % 4]["pp" + str(k // 4)][:])

        def out1_final(ps, k):
            o = work.tile([P, C], F32, tag="z" + str(k % 4), bufs=2)
            nc.vector.tensor_tensor(out=o[:], in0=ps[:], in1=parts[k], op=ALU.add)
            nc.sync.dma_start(out=out1_view[k % 4][:, k // 4 * 512 : (k // 4 + 1) * 512], in_=o[:])

        s_jobs = {}
        v_jobs = {}
        p_jobs = {}
        l_jobs = {}

        def add(dct, t, fn):
            dct.setdefault(t, []).append(fn)

        add(v_jobs, 0, lambda: quant_w(0))
        add(v_jobs, 0, lambda: quant_w(1))
        add(v_jobs, 0, lambda: ilv_w(2, "v"))
        add(v_jobs, 0, lambda: ilv_w(3, "v"))
        add(v_jobs, 0, lambda: quant_w(2))
        add(v_jobs, 1, lambda: quant_w(3))
        for g in range(4):
            it = X_AT[g]
            add(l_jobs, it - 1, lambda g=g: load_x(g))
            add(s_jobs, it, lambda g=g: ilv_x(g, "s"))
            add(v_jobs, it + 1, lambda g=g: quant_x(g))
            ih = H_AT[g]
            if g % 2 == 0:
                add(l_jobs, ih - 1, lambda g=g: load_hidden(g // 2))
            add(p_jobs, ih, lambda g=g: hid_tr(g))
            add(s_jobs, ih, lambda g=g: hid_evac(g))
            add(v_jobs, ih + 1, lambda g=g: quant_h(g))
        for g in range(3):
            tl = max(t for t in range(TILES) if st[t]["pa"] == g)
            add(p_jobs, tl + 1, lambda g=g: dft_tr(g))
            add(s_jobs, tl + 1, lambda g=g: dft_evac(g, "ss"))
            add(v_jobs, tl + 2, lambda g=g: quant_ft(g))

        for k in range(8):
            add(p_jobs, PART_AT[k], lambda k=k: out1_part_mm(k))
            add(s_jobs, PART_AT[k], lambda k=k: out1_part_evac(k))

        def run(dct, t):
            for fn in dct.get(t, []):
                fn()

        with tc.manual_schedule(engines={ENG.PE, ENG.Activation, ENG.DVE, ENG.Pool}):
            load_gate(0, 0)
            load_gate(0, 1)
            load_half(0, (0, 1))
            load_gate(0, 2)
            load_gate(0, 3)
            load_w(0)
            load_w(1)
            for gi in (0, 1, 2, 3):
                load_gate(1, gi)
            load_half(0, (1, 4))
            load_w(2)
            load_w(3)
            zi_tr(0)
            i_act(0)
            i_back(0)
            gh(0)
            acts(0)
            v_a(0)
            ilv_w(0, "v")
            ilv_w(1, "v")

            for t in range(TILES):
                if t + 2 < TILES:
                    if st[t + 2]["l"] == 0:
                        load_half(st[t + 2]["pa"], (0, 4))
                    for gi in (0, 1, 2, 3):
                        load_gate(t + 2, gi)
                run(l_jobs, t)
                if t > 0:
                    v_ndc(t - 1)
                    dz_f(t - 1, nc.gpsimd)
                    dz_i(t - 1, nc.gpsimd)
                    dz_g(t - 1, nc.gpsimd, 0, 1)
                    back(t - 1, "th")
                v_b(t)
                c_th(t)
                v_xi_xg(t)
                if t > 0:
                    dz_o(t - 1)
                v_go(t)
                if t > 0:
                    dz_g(t - 1, nc.vector, 1, 2)
                v_xf(t)
                v_y(t)
                if t + 1 < TILES:
                    zi_tr(t + 1)
                    i_act(t + 1)
                    act_sb(t + 1, 0, "f", ACT.Sigmoid)
                    acts_g(t + 1)
                if t > 1:
                    out0_mm(t - 2)
                    out0_evac(t - 2, "s")
                if t + 1 < TILES:
                    i_back(t + 1)
                    act_sb(t + 1, 3, "o", ACT.Sigmoid)
                    gh(t + 1)
                back(t, "sq")
                run(p_jobs, t)
                run(s_jobs, t)
                if t > 0:
                    quants(t - 1)
                run(v_jobs, t)
                if t + 1 < TILES:
                    v_a(t + 1)

            t = TILES
            v_ndc(t - 1)
            dz_f(t - 1, nc.vector)
            back(t - 1, "th")
            dft_tr(3)
            dft_evac(3, "ss")
            out0_mm(t - 2)
            out0_evac(t - 2, "s")
            dz_o(t - 1)
            dz_i(t - 1, nc.vector)
            dz_g(t - 1, nc.vector)
            tags = [("i", 2), ("i", 2), ("gh", 1), ("bk", 2), ("bk", 2), ("mm", 3), ("mm", 3), ("mm", 3)]
            banks = []
            for k in range(5):
                ps = psum.tile([P, 512], F32, tag=tags[k][0], bufs=tags[k][1])
                out1_mm(ps, k % 4, k // 4, 2, 3, 2, 3)
                banks.append(ps)
            run(v_jobs, t)
            quants(t - 1)
            out0_mm(t - 1)
            out0_evac(t - 1, "s")
            quant_ft(3)
            for k in range(8):
                if k < 5:
                    out1_mm(banks[k], k % 4, k // 4, 3, 4, 2, 3)
                    ps = banks[k]
                else:
                    ps = psum.tile([P, 512], F32, tag=tags[k][0], bufs=tags[k][1])
                    out1_mm(ps, k % 4, k // 4, 2, 4, 2, 3)
                out1_final(ps, k)
